import numpy as np
import ml_dtypes


def mxq(x, axis, fmt="e4m3"):
    dtype, down = {"e4m3": (ml_dtypes.float8_e4m3fn, 7), "e5m2": (ml_dtypes.float8_e5m2, 14)}[fmt]
    v = np.moveaxis(np.asarray(x, np.float32).astype(ml_dtypes.bfloat16).astype(np.float64), axis, -1)
    blocks = v.reshape(v.shape[:-1] + (-1, 32))
    amax = np.abs(blocks).max(-1, keepdims=True)
    byte = np.maximum(np.where(amax > 0, np.frexp(amax)[1] - 1 + 127, 0) - down, 1)
    scale = np.exp2(byte - 127.0)
    codes = (blocks / scale).astype(np.float32).astype(dtype).astype(np.float64)
    return np.moveaxis((codes * scale).reshape(v.shape), -1, axis)


WIDE = False


def mx_kscale(k):
    if not WIDE:
        return np.ones(k)
    levels = np.array([10, -10, 5, -5, 0])
    a = np.random.permutation(np.resize(levels, k // 512 * 4)).reshape(k // 512, 4)
    idx = np.arange(k)
    return np.exp2(a[idx // 512, idx % 128 // 32])


BF16 = ml_dtypes.bfloat16


def bf(x):
    return np.asarray(x, np.float32).astype(BF16)


def f64(x):
    return np.asarray(x).astype(np.float64)


NT, N, C_IN, C_H, C_OUT, ORDER = 8192, 512, 1024, 512, 256, 3


def setup_inputs():
    s = mx_kscale(C_IN)
    return {"nf_mats": bf(np.random.standard_normal((N, C_IN)) * s),
            "conv_mats": bf(np.random.standard_normal((NT, N)) / np.sqrt(N)),
            "W1": bf(np.random.standard_normal((C_IN, C_H)) / np.sqrt(C_IN) / s[:, None]),
            "b1": bf(np.random.standard_normal(C_H) * 0.2),
            "c1": bf(0.4 ** np.arange(ORDER) * (1.0 + 0.1 * np.random.standard_normal(ORDER)))}


def reference(nf_mats, conv_mats, W1, b1, c1):
    coeffs = f64(c1)
    h = (mxq(f64(nf_mats), 1, "e4m3") @ mxq(f64(W1), 0, "e4m3")) + f64(b1)
    z = mxq(f64(conv_mats), 1, "e4m3") @ mxq(h, 0, "e4m3")
    p = z
    acc = coeffs[0] * z
    for d in range(1, ORDER):
        p = p * z
        acc = acc + coeffs[d] * p
    return acc

@@ -1,0 +1,296 @@
+from contextlib import ExitStack
+
+import concourse.mybir as mybir
+from concourse.masks import make_identity
+
+F32 = mybir.dt.float32
+BF16 = mybir.dt.bfloat16
+U32 = mybir.dt.uint32
+U8 = mybir.dt.uint8
+FP8X4 = mybir.dt.float8_e4m3fn_x4
+ALU = mybir.AluOpType
+ACT = mybir.ActivationFunctionType
+
+P = 128
+NT, N, C_IN, C_H = 8192, 512, 1024, 512
+FLOPS = 2 * N * C_IN * C_H + 2 * NT * N * C_H
+
+CHUNKS = 8
+TILES = 8
+NPAIRS = 32
+KINDS = "KHKHKHQH"
+LEAD = 4
+VDELAY = 2
+MANUAL = True
+
+
+def tile_sketchgcn_pa_t_kernel(tc, nf_mats, conv_mats, W1, b1, c1, out):
+    nc = tc.nc
+    with ExitStack() as ctx:
+        const = ctx.enter_context(tc.tile_pool(name="const", bufs=1))
+        convp = ctx.enter_context(tc.tile_pool(name="convp", bufs=CHUNKS))
+        grpp = ctx.enter_context(tc.tile_pool(name="grpp", bufs=4))
+        codep = ctx.enter_context(tc.tile_pool(name="codep", bufs=4))
+        work = ctx.enter_context(tc.tile_pool(name="work", bufs=4))
+        outp = ctx.enter_context(tc.tile_pool(name="outp", bufs=4))
+        psum_t = ctx.enter_context(tc.psum_pool(name="psum_t", bufs=2))
+        psum_z = ctx.enter_context(tc.psum_pool(name="psum_z", bufs=6))
+        if MANUAL:
+            ctx.enter_context(tc.manual_schedule())
+
+        ident = const.tile([P, P], F32, name="ident")
+        make_identity(nc, ident[:])
+        cz = const.tile([P, 32], BF16, name="cz")
+        nc.vector.memset(cz[:], 0.0)
+        bz = const.tile([P, C_H], BF16, name="bz")
+        nc.vector.memset(bz[:], 0.0)
+        ones = const.tile([P, P], BF16, name="ones")
+        nc.vector.memset(ones[:], 1.0)
+        nc.sync.dma_start(out=cz[0:1, 0:3], in_=c1.rearrange("(o c) -> o c", o=1))
+        nc.sync.dma_start(out=bz[0:1, :], in_=b1.rearrange("(o c) -> o c", o=1))
+
+        nf_sb = const.tile([P, 4 * C_IN], BF16, name="nf_sb")
+        nf_v = nf_mats.rearrange("(u p e) k -> p u (e k)", u=2, p=P, e=2)
+        w_raw = const.tile([P, 4 * 2 * C_H], BF16, name="w_raw")
+        w_v = W1.rearrange("(a q e) c -> q a (e c)", a=4, q=P, e=2)
+        nc.sync.dma_start(out=nf_sb[:, 0:2048], in_=nf_v[:, 0, :])
+        nc.sync.dma_start(
+            out=w_raw[:, 0:2048].rearrange("q (a x) -> q a x", a=2), in_=w_v[:, 0:2, :]
+        )
+        nc.sync.dma_start(out=nf_sb[:, 2048:4096], in_=nf_v[:, 1, :])
+        nc.sync.dma_start(
+            out=w_raw[:, 2048:4096].rearrange("q (a x) -> q a x", a=2), in_=w_v[:, 2:4, :]
+        )
+        conv_v = conv_mats.rearrange("(g p j) n -> g p (j n)", g=CHUNKS, p=P, j=TILES)
+        out_v = out.rearrange("(g p j) c -> g p (j c)", g=CHUNKS, p=P, j=TILES)
+        conv_sb = []
+        for g in range(CHUNKS):
+            cs = convp.tile([P, TILES * N], BF16, name="conv%d" % g, tag="conv")
+            nc.sync.dma_start(out=cs[:], in_=conv_v[g])
+            conv_sb.append(cs)
+
+        def transpose_bank(src_words, offs, dst_words, engine):
+            bank = psum_t.tile([P, 512], F32, name="tp", tag="tp")
+            for jj in range(2):
+                for u in range(2):
+                    col = (2 * jj + u) * P
+                    nc.tensor.transpose(
+                        bank[:, col : col + P],
+                        src_words[:, offs[jj] + P * u : offs[jj] + P * (u + 1)],
+                        ident[:],
+                    )
+            dst = dst_words.rearrange("p (jj m u) -> p jj m u", jj=2, u=2)
+            src = bank[:].rearrange("p (jj u m) -> p jj m u", jj=2, u=2)
+            if engine == "V":
+                nc.vector.tensor_copy(out=dst, in_=src)
+            else:
+                nc.scalar.copy(out=dst, in_=src)
+
+        def regroup(dst, src):
+            nc.vector.tensor_copy(
+                out=dst.rearrange("p (c i t) -> p c t i", i=4, t=4),
+                in_=src.rearrange("p (t c i) -> p c t i", t=4, i=4),
+            )
+
+        nf_words = nf_sb[:].bitcast(F32)
+        nf_grp = const.tile([P, 4096], BF16, name="nf_grp", align_bytes=64)
+        nf_grp_words = nf_grp[:].bitcast(F32)
+        nf_codes = const.tile([P, 1024], U32, name="nf_codes", align_bytes=64)
+        nf_scales = const.tile([P, 1024], U8, name="nf_scales", align_bytes=64)
+        w_grp = const.tile([P, 4096], BF16, name="w_grp", align_bytes=64)
+        w_codes = const.tile([P, 1024], U32, name="w_codes", align_bytes=64)
+        w_scales = const.tile([P, 1024], U8, name="w_scales", align_bytes=64)
+
+        def nf_half(jp):
+            for g in range(2):
+                offs = [(2 * jp + jj) * 512 + g * 256 for jj in range(2)]
+                s0 = jp * 4 + g * 2
+                transpose_bank(nf_words, offs, nf_grp_words[:, s0 * 256 : s0 * 256 + 512], "S")
+
+        def nf_quant(jp):
+            nc.vector.quantize_mx(
+                out=nf_codes[:, jp * 512 : (jp + 1) * 512].bitcast(FP8X4),
+                scales=nf_scales[:, jp * 512 : (jp + 1) * 512],
+                in_=nf_grp[:, jp * 2048 : (jp + 1) * 2048],
+            )
+
+        def w_quant(g):
+            nc.vector.quantize_mx(
+                out=w_codes[:, g * 512 : (g + 1) * 512].bitcast(FP8X4),
+                scales=w_scales[:, g * 512 : (g + 1) * 512],
+                in_=w_grp[:, g * 2048 : (g + 1) * 2048],
+            )
+
+        nf_half(0)
+        regroup(w_grp[:, 0:2048], w_raw[:, 0:2048])
+        nf_quant(0)
+        nf_half(1)
+        w_quant(0)
+        regroup(w_grp[:, 2048:4096], w_raw[:, 2048:4096])
+        nf_quant(1)
+        w_quant(1)
+
+        pc = psum_z.tile([P, 512], F32, name="pc", tag="z")
+        nc.tensor.matmul(out=pc[:, 0:32], lhsT=ones[:], rhs=cz[:], start=True, stop=True)
+        cf = const.tile([P, 32], F32, name="cf")
+        nc.scalar.activation(out=cf[:], in_=pc[:, 0:32], func=ACT.Identity)
+        pb = psum_z.tile([P, 512], F32, name="pb", tag="z")
+        nc.tensor.matmul(out=pb[:], lhsT=ones[:], rhs=bz[:], start=True, stop=True)
+        b1f = const.tile([P, C_H], F32, name="b1f")
+        nc.scalar.copy(out=b1f[:], in_=pb[:])
+        c0 = cf[:, 0:1]
+        c1s = cf[:, 1:2]
+        c2 = cf[:, 2:3]
+
+        codes = {}
+        groups = {}
+
+        def prep_bank(k):
+            g = k // 4
+            b = k % 4
+            if b == 0:
+                cc = codep.tile([P, 1024], U32, name="cc%d" % g, tag="cc", align_bytes=64)
+                sc = codep.tile([P, 1024], U8, name="sc%d" % g, tag="sc", align_bytes=64)
+                codes[g] = (cc, sc)
+            if b % 2 == 0:
+                grp = grpp.tile([P, 2048], BF16, name="grp", tag="grp", align_bytes=64)
+                groups[k // 2] = grp
+            grp_words = groups[k // 2][:].bitcast(F32)
+            words = conv_sb[g][:].bitcast(F32)
+            j0 = 2 * b
+            lo = (b % 2) * 512
+            transpose_bank(words, [j0 * 256, (j0 + 1) * 256], grp_words[:, lo : lo + 512], "S")
+
+        def quantise_half(r):
+            g = r // 2
+            hh = r % 2
+            cc, sc = codes[g]
+            nc.vector.quantize_mx(
+                out=cc[:, hh * 512 : (hh + 1) * 512].bitcast(FP8X4),
+                scales=sc[:, hh * 512 : (hh + 1) * 512],
+                in_=groups[r][:],
+            )
+
+        prep_bank(0)
+        prep_bank(1)
+        quantise_half(0)
+
+        h_grp = const.tile([P, 4 * C_H], BF16, name="h_grp", align_bytes=64)
+        h_codes = const.tile([P, C_H], U32, name="h_codes", align_bytes=64)
+        h_scales = const.tile([P, C_H], U8, name="h_scales", align_bytes=64)
+
+        def h_quant(b):
+            nc.vector.quantize_mx(
+                out=h_codes[:, b * P : (b + 1) * P].bitcast(FP8X4),
+                scales=h_scales[:, b * P : (b + 1) * P],
+                in_=h_grp[:, b * 512 : (b + 1) * 512],
+            )
+
+        for b in range(4):
+            acc = psum_z.tile([P, 512], F32, name="acc", tag="z")
+            for j in range(4):
+                for g in range(2):
+                    s = (j // 2) * 4 + g * 2 + (j % 2)
+                    cols = slice(g * 512 + b * P, g * 512 + (b + 1) * P)
+                    nc.tensor.matmul_mx(
+                        out=acc[:, j * P : (j + 1) * P],
+                        lhsT=nf_codes[:, s * P : (s + 1) * P].bitcast(FP8X4),
+                        lhsT_scale=nf_scales[:, s * P : (s + 1) * P],
+                        rhs=w_codes[:, cols].bitcast(FP8X4),
+                        rhs_scale=w_scales[:, cols],
+                        start=(g == 0),
+                        stop=(g == 1),
+                    )
+            nc.vector.tensor_tensor(
+                out=h_grp[:, b * 512 : (b + 1) * 512].rearrange("p (c j) -> p c j", j=4),
+                in0=acc[:].rearrange("p (j c) -> p c j", j=4),
+                in1=b1f[:, b * P : (b + 1) * P].unsqueeze(2).to_broadcast([P, P, 4]),
+                op=ALU.add,
+            )
+            if b >= 1:
+                h_quant(b - 1)
+        h_quant(3)
+
+        for k in range(2, LEAD):
+            prep_bank(k)
+            if k % 2 == 1:
+                quantise_half(k // 2)
+
+        halves = [slice(0, 512), slice(512, 1024)]
+        state = {}
+
+        def multiply(i):
+            cc, sc = codes[i // 4]
+            banks = []
+            for jj in range(2):
+                j = 2 * (i % 4) + jj
+                z = psum_z.tile([P, 512], F32, name="z", tag="z")
+                nc.tensor.matmul_mx(
+                    out=z[:],
+                    lhsT=cc[:, j * P : (j + 1) * P].bitcast(FP8X4),
+                    lhsT_scale=sc[:, j * P : (j + 1) * P],
+                    rhs=h_codes[:].bitcast(FP8X4),
+                    rhs_scale=h_scales[:],
+                    start=True,
+                    stop=True,
+                )
+                banks.append(z)
+            return banks
+
+        def affine(tu, banks):
+            for jj in range(2):
+                nc.scalar.activation(
+                    out=tu[:, halves[jj]], in_=banks[jj][:], func=ACT.Identity, bias=c1s, scale=c2
+                )
+
+        def start_pair(i):
+            kind = KINDS[i % len(KINDS)]
+            banks = multiply(i)
+            tu = work.tile([P, 1024], F32, name="tu", tag="tu")
+            if kind == "H":
+                affine(tu, banks)
+            else:
+                zs = work.tile([P, 1024], F32, name="zs", tag="zs")
+                for jj in range(2):
+                    nc.scalar.copy(out=zs[:, halves[jj]], in_=banks[jj][:])
+                if kind == "Q":
+                    affine(tu, banks)
+                else:
+                    nc.gpsimd.tensor_scalar(
+                        out=tu[:], in0=zs[:], scalar1=c2, scalar2=c1s, op0=ALU.mult, op1=ALU.add
+                    )
+                nc.gpsimd.tensor_tensor(out=tu[:], in0=tu[:], in1=zs[:], op=ALU.mult)
+            state[i] = (tu, banks)
+
+        def finish_pair(i):
+            kind = KINDS[i % len(KINDS)]
+            tu, banks = state[i]
+            if kind != "H":
+                banks = multiply(i)
+            o = outp.tile([P, 1024], F32, name="o", tag="o")
+            if kind == "H":
+                for jj in range(2):
+                    nc.vector.tensor_tensor(
+                        out=tu[:, halves[jj]], in0=tu[:, halves[jj]], in1=banks[jj][:], op=ALU.mult
+                    )
+            for jj in range(2):
+                nc.vector.scalar_tensor_tensor(
+                    out=o[:, halves[jj]], in0=tu[:, halves[jj]], scalar=c0, in1=banks[jj][:],
+                    op0=ALU.add, op1=ALU.mult,
+                )
+            b = i % 4
+            nc.sync.dma_start(out=out_v[i // 4][:, b * 1024 : (b + 1) * 1024], in_=o[:])
+
+        for i in range(NPAIRS + VDELAY):
+            k = LEAD + i
+            if k < NPAIRS:
+                prep_bank(k)
+            if i < NPAIRS:
+                start_pair(i)
+                if KINDS[i % len(KINDS)] == "H":
+                    finish_pair(i)
+            d = i - VDELAY
+            if d >= 0 and KINDS[d % len(KINDS)] != "H":
+                finish_pair(d)
+            if k < NPAIRS and k % 2 == 1:
+                quantise_half(k // 2)

@@ -18,8 +18,8 @@ FLOPS = 2 * N * C_IN * C_H + 2 * NT * N * C_H
 CHUNKS = 8
 TILES = 8
 NPAIRS = 32
-KINDS = "KHKHKHQH"
-LEAD = 4
+KINDS = "HHHH" + "KHQH" * 7
+LEAD = 5
 VDELAY = 2
 MANUAL = True
 
@@ -173,7 +173,6 @@ def tile_sketchgcn_pa_t_kernel(tc, nf_mats, conv_mats, W1, b1, c1, out):
 
         prep_bank(0)
         prep_bank(1)
-        quantise_half(0)
 
         h_grp = const.tile([P, 4 * C_H], BF16, name="h_grp", align_bytes=64)
         h_codes = const.tile([P, C_H], U32, name="h_codes", align_bytes=64)
@@ -207,7 +206,9 @@ def tile_sketchgcn_pa_t_kernel(tc, nf_mats, conv_mats, W1, b1, c1, out):
                 in1=b1f[:, b * P : (b + 1) * P].unsqueeze(2).to_broadcast([P, P, 4]),
                 op=ALU.add,
             )
-            if b >= 1:
+            if b == 0:
+                quantise_half(0)
+            else:
                 h_quant(b - 1)
         h_quant(3)
 
@@ -244,7 +245,7 @@ def tile_sketchgcn_pa_t_kernel(tc, nf_mats, conv_mats, W1, b1, c1, out):
                 )
 
         def start_pair(i):
-            kind = KINDS[i % len(KINDS)]
+            kind = KINDS[i]
             banks = multiply(i)
             tu = work.tile([P, 1024], F32, name="tu", tag="tu")
             if kind == "H":
@@ -263,7 +264,7 @@ def tile_sketchgcn_pa_t_kernel(tc, nf_mats, conv_mats, W1, b1, c1, out):
             state[i] = (tu, banks)
 
         def finish_pair(i):
-            kind = KINDS[i % len(KINDS)]
+            kind = KINDS[i]
             tu, banks = state[i]
             if kind != "H":
                 banks = multiply(i)
@@ -279,18 +280,23 @@ def tile_sketchgcn_pa_t_kernel(tc, nf_mats, conv_mats, W1, b1, c1, out):
                     op0=ALU.add, op1=ALU.mult,
                 )
             b = i % 4
-            nc.sync.dma_start(out=out_v[i // 4][:, b * 1024 : (b + 1) * 1024], in_=o[:])
+            if i >= NPAIRS - 2:
+                for jj in range(2):
+                    lo = b * 1024 + jj * 512
+                    nc.sync.dma_start(out=out_v[i // 4][:, lo : lo + 512], in_=o[:, halves[jj]])
+            else:
+                nc.sync.dma_start(out=out_v[i // 4][:, b * 1024 : (b + 1) * 1024], in_=o[:])
 
         for i in range(NPAIRS + VDELAY):
             k = LEAD + i
             if k < NPAIRS:
                 prep_bank(k)
+                if k % 2 == 1:
+                    quantise_half(k // 2)
             if i < NPAIRS:
                 start_pair(i)
-                if KINDS[i % len(KINDS)] == "H":
+                if KINDS[i] == "H":
                     finish_pair(i)
             d = i - VDELAY
-            if d >= 0 and KINDS[d % len(KINDS)] != "H":
+            if d >= 0 and KINDS[d] != "H":
                 finish_pair(d)
-            if k < NPAIRS and k % 2 == 1:
-                quantise_half(k // 2)

@@ -18,10 +18,11 @@ FLOPS = 2 * N * C_IN * C_H + 2 * NT * N * C_H
 CHUNKS = 8
 TILES = 8
 NPAIRS = 32
-KINDS = "HHHH" + "KHQH" * 7
-LEAD = 5
+KINDS = "KHKHKHQH"
+LEAD = 4
 VDELAY = 2
 MANUAL = True
+WARM = 2
 
 
 def tile_sketchgcn_pa_t_kernel(tc, nf_mats, conv_mats, W1, b1, c1, out):
@@ -69,8 +70,21 @@ def tile_sketchgcn_pa_t_kernel(tc, nf_mats, conv_mats, W1, b1, c1, out):
             nc.sync.dma_start(out=cs[:], in_=conv_v[g])
             conv_sb.append(cs)
 
-        def transpose_bank(src_words, offs, dst_words, engine):
+        def warm_passes(bank, n):
+            for r in range(n):
+                nc.tensor.matmul_mx(
+                    out=bank[:],
+                    lhsT=h_codes[:, 0:P].bitcast(FP8X4),
+                    lhsT_scale=h_scales[:, 0:P],
+                    rhs=h_codes[:].bitcast(FP8X4),
+                    rhs_scale=h_scales[:],
+                    start=True,
+                    stop=True,
+                )
+
+        def transpose_bank(src_words, offs, dst_words, engine, warm=0):
             bank = psum_t.tile([P, 512], F32, name="tp", tag="tp")
+            warm_passes(bank, warm)
             for jj in range(2):
                 for u in range(2):
                     col = (2 * jj + u) * P
@@ -145,7 +159,7 @@ def tile_sketchgcn_pa_t_kernel(tc, nf_mats, conv_mats, W1, b1, c1, out):
         codes = {}
         groups = {}
 
-        def prep_bank(k):
+        def prep_bank(k, warm=0):
             g = k // 4
             b = k % 4
             if b == 0:
@@ -159,7 +173,9 @@ def tile_sketchgcn_pa_t_kernel(tc, nf_mats, conv_mats, W1, b1, c1, out):
             words = conv_sb[g][:].bitcast(F32)
             j0 = 2 * b
             lo = (b % 2) * 512
-            transpose_bank(words, [j0 * 256, (j0 + 1) * 256], grp_words[:, lo : lo + 512], "S")
+            transpose_bank(
+                words, [j0 * 256, (j0 + 1) * 256], grp_words[:, lo : lo + 512], "S", warm
+            )
 
         def quantise_half(r):
             g = r // 2
@@ -173,6 +189,7 @@ def tile_sketchgcn_pa_t_kernel(tc, nf_mats, conv_mats, W1, b1, c1, out):
 
         prep_bank(0)
         prep_bank(1)
+        quantise_half(0)
 
         h_grp = const.tile([P, 4 * C_H], BF16, name="h_grp", align_bytes=64)
         h_codes = const.tile([P, C_H], U32, name="h_codes", align_bytes=64)
@@ -206,9 +223,7 @@ def tile_sketchgcn_pa_t_kernel(tc, nf_mats, conv_mats, W1, b1, c1, out):
                 in1=b1f[:, b * P : (b + 1) * P].unsqueeze(2).to_broadcast([P, P, 4]),
                 op=ALU.add,
             )
-            if b == 0:
-                quantise_half(0)
-            else:
+            if b >= 1:
                 h_quant(b - 1)
         h_quant(3)
 
@@ -245,7 +260,7 @@ def tile_sketchgcn_pa_t_kernel(tc, nf_mats, conv_mats, W1, b1, c1, out):
                 )
 
         def start_pair(i):
-            kind = KINDS[i]
+            kind = KINDS[i % len(KINDS)]
             banks = multiply(i)
             tu = work.tile([P, 1024], F32, name="tu", tag="tu")
             if kind == "H":
@@ -264,7 +279,7 @@ def tile_sketchgcn_pa_t_kernel(tc, nf_mats, conv_mats, W1, b1, c1, out):
             state[i] = (tu, banks)
 
         def finish_pair(i):
-            kind = KINDS[i]
+            kind = KINDS[i % len(KINDS)]
             tu, banks = state[i]
             if kind != "H":
                 banks = multiply(i)
@@ -280,23 +295,23 @@ def tile_sketchgcn_pa_t_kernel(tc, nf_mats, conv_mats, W1, b1, c1, out):
                     op0=ALU.add, op1=ALU.mult,
                 )
             b = i % 4
-            if i >= NPAIRS - 2:
-                for jj in range(2):
-                    lo = b * 1024 + jj * 512
-                    nc.sync.dma_start(out=out_v[i // 4][:, lo : lo + 512], in_=o[:, halves[jj]])
-            else:
-                nc.sync.dma_start(out=out_v[i // 4][:, b * 1024 : (b + 1) * 1024], in_=o[:])
+            nc.sync.dma_start(out=out_v[i // 4][:, b * 1024 : (b + 1) * 1024], in_=o[:])
 
         for i in range(NPAIRS + VDELAY):
             k = LEAD + i
+            d = i - VDELAY
+            repeats = d >= 0 and KINDS[d % len(KINDS)] != "H"
+            warm = 0 if repeats else WARM
             if k < NPAIRS:
-                prep_bank(k)
-                if k % 2 == 1:
-                    quantise_half(k // 2)
+                prep_bank(k, warm)
+            elif warm > 0 and i < NPAIRS:
+                spare = psum_t.tile([P, 512], F32, name="spare", tag="tp")
+                warm_passes(spare, warm)
             if i < NPAIRS:
                 start_pair(i)
-                if KINDS[i] == "H":
+                if KINDS[i % len(KINDS)] == "H":
                     finish_pair(i)
-            d = i - VDELAY
-            if d >= 0 and KINDS[d] != "H":
+            if repeats:
                 finish_pair(d)
+            if k < NPAIRS and k % 2 == 1:
+                quantise_half(k // 2)

@@ -18,11 +18,10 @@ FLOPS = 2 * N * C_IN * C_H + 2 * NT * N * C_H
 CHUNKS = 8
 TILES = 8
 NPAIRS = 32
-KINDS = "KHKHKHQH"
+KINDS = "KHKH"
 LEAD = 4
 VDELAY = 2
 MANUAL = True
-WARM = 2
 
 
 def tile_sketchgcn_pa_t_kernel(tc, nf_mats, conv_mats, W1, b1, c1, out):
@@ -70,21 +69,8 @@ def tile_sketchgcn_pa_t_kernel(tc, nf_mats, conv_mats, W1, b1, c1, out):
             nc.sync.dma_start(out=cs[:], in_=conv_v[g])
             conv_sb.append(cs)
 
-        def warm_passes(bank, n):
-            for r in range(n):
-                nc.tensor.matmul_mx(
-                    out=bank[:],
-                    lhsT=h_codes[:, 0:P].bitcast(FP8X4),
-                    lhsT_scale=h_scales[:, 0:P],
-                    rhs=h_codes[:].bitcast(FP8X4),
-                    rhs_scale=h_scales[:],
-                    start=True,
-                    stop=True,
-                )
-
-        def transpose_bank(src_words, offs, dst_words, engine, warm=0):
+        def transpose_bank(src_words, offs, dst_words, engine):
             bank = psum_t.tile([P, 512], F32, name="tp", tag="tp")
-            warm_passes(bank, warm)
             for jj in range(2):
                 for u in range(2):
                     col = (2 * jj + u) * P
@@ -159,7 +145,7 @@ def tile_sketchgcn_pa_t_kernel(tc, nf_mats, conv_mats, W1, b1, c1, out):
         codes = {}
         groups = {}
 
-        def prep_bank(k, warm=0):
+        def prep_bank(k):
             g = k // 4
             b = k % 4
             if b == 0:
@@ -173,9 +159,7 @@ def tile_sketchgcn_pa_t_kernel(tc, nf_mats, conv_mats, W1, b1, c1, out):
             words = conv_sb[g][:].bitcast(F32)
             j0 = 2 * b
             lo = (b % 2) * 512
-            transpose_bank(
-                words, [j0 * 256, (j0 + 1) * 256], grp_words[:, lo : lo + 512], "S", warm
-            )
+            transpose_bank(words, [j0 * 256, (j0 + 1) * 256], grp_words[:, lo : lo + 512], "S")
 
         def quantise_half(r):
             g = r // 2
@@ -299,19 +283,14 @@ def tile_sketchgcn_pa_t_kernel(tc, nf_mats, conv_mats, W1, b1, c1, out):
 
         for i in range(NPAIRS + VDELAY):
             k = LEAD + i
-            d = i - VDELAY
-            repeats = d >= 0 and KINDS[d % len(KINDS)] != "H"
-            warm = 0 if repeats else WARM
             if k < NPAIRS:
-                prep_bank(k, warm)
-            elif warm > 0 and i < NPAIRS:
-                spare = psum_t.tile([P, 512], F32, name="spare", tag="tp")
-                warm_passes(spare, warm)
+                prep_bank(k)
             if i < NPAIRS:
                 start_pair(i)
                 if KINDS[i % len(KINDS)] == "H":
                     finish_pair(i)
-            if repeats:
+            d = i - VDELAY
+            if d >= 0 and KINDS[d % len(KINDS)] != "H":
                 finish_pair(d)
             if k < NPAIRS and k % 2 == 1:
                 quantise_half(k // 2)

@@ -18,8 +18,8 @@ FLOPS = 2 * N * C_IN * C_H + 2 * NT * N * C_H
 CHUNKS = 8
 TILES = 8
 NPAIRS = 32
-KINDS = "KHKH"
-LEAD = 4
+KINDS = "HHHH" + "KHQH" * 7
+LEAD = 5
 VDELAY = 2
 MANUAL = True
 
@@ -173,7 +173,6 @@ def tile_sketchgcn_pa_t_kernel(tc, nf_mats, conv_mats, W1, b1, c1, out):
 
         prep_bank(0)
         prep_bank(1)
-        quantise_half(0)
 
         h_grp = const.tile([P, 4 * C_H], BF16, name="h_grp", align_bytes=64)
         h_codes = const.tile([P, C_H], U32, name="h_codes", align_bytes=64)
@@ -207,7 +206,9 @@ def tile_sketchgcn_pa_t_kernel(tc, nf_mats, conv_mats, W1, b1, c1, out):
                 in1=b1f[:, b * P : (b + 1) * P].unsqueeze(2).to_broadcast([P, P, 4]),
                 op=ALU.add,
             )
-            if b >= 1:
+            if b == 0:
+                quantise_half(0)
+            else:
                 h_quant(b - 1)
         h_quant(3)
 
@@ -244,11 +245,14 @@ def tile_sketchgcn_pa_t_kernel(tc, nf_mats, conv_mats, W1, b1, c1, out):
                 )
 
         def start_pair(i):
-            kind = KINDS[i % len(KINDS)]
+            kind = KINDS[i]
             banks = multiply(i)
             tu = work.tile([P, 1024], F32, name="tu", tag="tu")
             if kind == "H":
-                affine(tu, banks)
+                for jj in range(2):
+                    nc.scalar.activation(
+                        out=tu[:, halves[jj]], in_=banks[jj][:], func=ACT.Copy, scale=c2
+                    )
             else:
                 zs = work.tile([P, 1024], F32, name="zs", tag="zs")
                 for jj in range(2):
@@ -263,15 +267,16 @@ def tile_sketchgcn_pa_t_kernel(tc, nf_mats, conv_mats, W1, b1, c1, out):
             state[i] = (tu, banks)
 
         def finish_pair(i):
-            kind = KINDS[i % len(KINDS)]
+            kind = KINDS[i]
             tu, banks = state[i]
             if kind != "H":
                 banks = multiply(i)
             o = outp.tile([P, 1024], F32, name="o", tag="o")
             if kind == "H":
                 for jj in range(2):
-                    nc.vector.tensor_tensor(
-                        out=tu[:, halves[jj]], in0=tu[:, halves[jj]], in1=banks[jj][:], op=ALU.mult
+                    nc.vector.scalar_tensor_tensor(
+                        out=tu[:, halves[jj]], in0=tu[:, halves[jj]], scalar=c1s, in1=banks[jj][:],
+                        op0=ALU.add, op1=ALU.mult,
                     )
             for jj in range(2):
                 nc.vector.scalar_tensor_tensor(
@@ -279,18 +284,23 @@ def tile_sketchgcn_pa_t_kernel(tc, nf_mats, conv_mats, W1, b1, c1, out):
                     op0=ALU.add, op1=ALU.mult,
                 )
             b = i % 4
-            nc.sync.dma_start(out=out_v[i // 4][:, b * 1024 : (b + 1) * 1024], in_=o[:])
+            if i >= NPAIRS - 2:
+                for jj in range(2):
+                    lo = b * 1024 + jj * 512
+                    nc.sync.dma_start(out=out_v[i // 4][:, lo : lo + 512], in_=o[:, halves[jj]])
+            else:
+                nc.sync.dma_start(out=out_v[i // 4][:, b * 1024 : (b + 1) * 1024], in_=o[:])
 
         for i in range(NPAIRS + VDELAY):
             k = LEAD + i
             if k < NPAIRS:
                 prep_bank(k)
+                if k % 2 == 1:
+                    quantise_half(k // 2)
             if i < NPAIRS:
                 start_pair(i)
-                if KINDS[i % len(KINDS)] == "H":
+                if KINDS[i] == "H":
                     finish_pair(i)
             d = i - VDELAY
-            if d >= 0 and KINDS[d % len(KINDS)] != "H":
+            if d >= 0 and KINDS[d] != "H":
                 finish_pair(d)
-            if k < NPAIRS and k % 2 == 1:
-                quantise_half(k // 2)

@@ -18,8 +18,8 @@ FLOPS = 2 * N * C_IN * C_H + 2 * NT * N * C_H
 CHUNKS = 8
 TILES = 8
 NPAIRS = 32
-KINDS = "HHHH" + "KHQH" * 7
-LEAD = 5
+KINDS = "KHQH"
+LEAD = 4
 VDELAY = 2
 MANUAL = True
 
@@ -173,6 +173,7 @@ def tile_sketchgcn_pa_t_kernel(tc, nf_mats, conv_mats, W1, b1, c1, out):
 
         prep_bank(0)
         prep_bank(1)
+        quantise_half(0)
 
         h_grp = const.tile([P, 4 * C_H], BF16, name="h_grp", align_bytes=64)
         h_codes = const.tile([P, C_H], U32, name="h_codes", align_bytes=64)
@@ -206,9 +207,7 @@ def tile_sketchgcn_pa_t_kernel(tc, nf_mats, conv_mats, W1, b1, c1, out):
                 in1=b1f[:, b * P : (b + 1) * P].unsqueeze(2).to_broadcast([P, P, 4]),
                 op=ALU.add,
             )
-            if b == 0:
-                quantise_half(0)
-            else:
+            if b >= 1:
                 h_quant(b - 1)
         h_quant(3)
 
@@ -245,14 +244,11 @@ def tile_sketchgcn_pa_t_kernel(tc, nf_mats, conv_mats, W1, b1, c1, out):
                 )
 
         def start_pair(i):
-            kind = KINDS[i]
+            kind = KINDS[i % len(KINDS)]
             banks = multiply(i)
             tu = work.tile([P, 1024], F32, name="tu", tag="tu")
             if kind == "H":
-                for jj in range(2):
-                    nc.scalar.activation(
-                        out=tu[:, halves[jj]], in_=banks[jj][:], func=ACT.Copy, scale=c2
-                    )
+                affine(tu, banks)
             else:
                 zs = work.tile([P, 1024], F32, name="zs", tag="zs")
                 for jj in range(2):
@@ -267,16 +263,15 @@ def tile_sketchgcn_pa_t_kernel(tc, nf_mats, conv_mats, W1, b1, c1, out):
             state[i] = (tu, banks)
 
         def finish_pair(i):
-            kind = KINDS[i]
+            kind = KINDS[i % len(KINDS)]
             tu, banks = state[i]
             if kind != "H":
                 banks = multiply(i)
             o = outp.tile([P, 1024], F32, name="o", tag="o")
             if kind == "H":
                 for jj in range(2):
-                    nc.vector.scalar_tensor_tensor(
-                        out=tu[:, halves[jj]], in0=tu[:, halves[jj]], scalar=c1s, in1=banks[jj][:],
-                        op0=ALU.add, op1=ALU.mult,
+                    nc.vector.tensor_tensor(
+                        out=tu[:, halves[jj]], in0=tu[:, halves[jj]], in1=banks[jj][:], op=ALU.mult
                     )
             for jj in range(2):
                 nc.vector.scalar_tensor_tensor(
@@ -284,23 +279,18 @@ def tile_sketchgcn_pa_t_kernel(tc, nf_mats, conv_mats, W1, b1, c1, out):
                     op0=ALU.add, op1=ALU.mult,
                 )
             b = i % 4
-            if i >= NPAIRS - 2:
-                for jj in range(2):
-                    lo = b * 1024 + jj * 512
-                    nc.sync.dma_start(out=out_v[i // 4][:, lo : lo + 512], in_=o[:, halves[jj]])
-            else:
-                nc.sync.dma_start(out=out_v[i // 4][:, b * 1024 : (b + 1) * 1024], in_=o[:])
+            nc.sync.dma_start(out=out_v[i // 4][:, b * 1024 : (b + 1) * 1024], in_=o[:])
 
         for i in range(NPAIRS + VDELAY):
             k = LEAD + i
             if k < NPAIRS:
                 prep_bank(k)
-                if k % 2 == 1:
-                    quantise_half(k // 2)
             if i < NPAIRS:
                 start_pair(i)
-                if KINDS[i] == "H":
+                if KINDS[i % len(KINDS)] == "H":
                     finish_pair(i)
             d = i - VDELAY
-            if d >= 0 and KINDS[d] != "H":
+            if d >= 0 and KINDS[d % len(KINDS)] != "H":
                 finish_pair(d)
+            if k < NPAIRS and k % 2 == 1:
+                quantise_half(k // 2)

@@ -18,10 +18,7 @@ FLOPS = 2 * N * C_IN * C_H + 2 * NT * N * C_H
 CHUNKS = 8
 TILES = 8
 NPAIRS = 32
-KINDS = "KHQH"
-LEAD = 4
-VDELAY = 2
-MANUAL = True
+VCOPY = (11, 19, 27)
 
 
 def tile_sketchgcn_pa_t_kernel(tc, nf_mats, conv_mats, W1, b1, c1, out):
@@ -29,14 +26,14 @@ def tile_sketchgcn_pa_t_kernel(tc, nf_mats, conv_mats, W1, b1, c1, out):
     with ExitStack() as ctx:
         const = ctx.enter_context(tc.tile_pool(name="const", bufs=1))
         convp = ctx.enter_context(tc.tile_pool(name="convp", bufs=CHUNKS))
-        grpp = ctx.enter_context(tc.tile_pool(name="grpp", bufs=4))
-        codep = ctx.enter_context(tc.tile_pool(name="codep", bufs=4))
-        work = ctx.enter_context(tc.tile_pool(name="work", bufs=4))
+        grpp = ctx.enter_context(tc.tile_pool(name="grpp", bufs=2))
+        codep = ctx.enter_context(tc.tile_pool(name="codep", bufs=CHUNKS))
+        work = ctx.enter_context(tc.tile_pool(name="work", bufs=3))
         outp = ctx.enter_context(tc.tile_pool(name="outp", bufs=4))
-        psum_t = ctx.enter_context(tc.psum_pool(name="psum_t", bufs=2))
-        psum_z = ctx.enter_context(tc.psum_pool(name="psum_z", bufs=6))
-        if MANUAL:
-            ctx.enter_context(tc.manual_schedule())
+        psum_h = ctx.enter_context(tc.psum_pool(name="psum_h", bufs=4))
+        psum_q = ctx.enter_context(tc.psum_pool(name="psum_q", bufs=2))
+        psum_r = ctx.enter_context(tc.psum_pool(name="psum_r", bufs=2))
+        ctx.enter_context(tc.manual_schedule())
 
         ident = const.tile([P, P], F32, name="ident")
         make_identity(nc, ident[:])
@@ -46,31 +43,36 @@ def tile_sketchgcn_pa_t_kernel(tc, nf_mats, conv_mats, W1, b1, c1, out):
         nc.vector.memset(bz[:], 0.0)
         ones = const.tile([P, P], BF16, name="ones")
         nc.vector.memset(ones[:], 1.0)
-        nc.sync.dma_start(out=cz[0:1, 0:3], in_=c1.rearrange("(o c) -> o c", o=1))
-        nc.sync.dma_start(out=bz[0:1, :], in_=b1.rearrange("(o c) -> o c", o=1))
-
         nf_sb = const.tile([P, 4 * C_IN], BF16, name="nf_sb")
         nf_v = nf_mats.rearrange("(u p e) k -> p u (e k)", u=2, p=P, e=2)
         w_raw = const.tile([P, 4 * 2 * C_H], BF16, name="w_raw")
         w_v = W1.rearrange("(a q e) c -> q a (e c)", a=4, q=P, e=2)
-        nc.sync.dma_start(out=nf_sb[:, 0:2048], in_=nf_v[:, 0, :])
-        nc.sync.dma_start(
-            out=w_raw[:, 0:2048].rearrange("q (a x) -> q a x", a=2), in_=w_v[:, 0:2, :]
-        )
-        nc.sync.dma_start(out=nf_sb[:, 2048:4096], in_=nf_v[:, 1, :])
-        nc.sync.dma_start(
-            out=w_raw[:, 2048:4096].rearrange("q (a x) -> q a x", a=2), in_=w_v[:, 2:4, :]
-        )
+        for u in range(2):
+            nc.sync.dma_start(
+                out=w_raw[:, u * 2048 : (u + 1) * 2048].rearrange("q (a x) -> q a x", a=2),
+                in_=w_v[:, 2 * u : 2 * u + 2, :],
+            )
+        for u in range(2):
+            nc.sync.dma_start(out=nf_sb[:, u * 2048 : (u + 1) * 2048], in_=nf_v[:, u, :])
+        nc.sync.dma_start(out=cz[0:1, 0:3], in_=c1.rearrange("(o c) -> o c", o=1))
+        nc.sync.dma_start(out=bz[0:1, :], in_=b1.rearrange("(o c) -> o c", o=1))
         conv_v = conv_mats.rearrange("(g p j) n -> g p (j n)", g=CHUNKS, p=P, j=TILES)
         out_v = out.rearrange("(g p j) c -> g p (j c)", g=CHUNKS, p=P, j=TILES)
         conv_sb = []
         for g in range(CHUNKS):
             cs = convp.tile([P, TILES * N], BF16, name="conv%d" % g, tag="conv")
-            nc.sync.dma_start(out=cs[:], in_=conv_v[g])
+            parts = 2 if g == 0 else 1
+            w = TILES * N // parts
+            for u in range(parts):
+                nc.sync.dma_start(out=cs[:, u * w : (u + 1) * w], in_=conv_v[g][:, u * w : (u + 1) * w])
             conv_sb.append(cs)
 
+        turn = [0]
+
         def transpose_bank(src_words, offs, dst_words, engine):
-            bank = psum_t.tile([P, 512], F32, name="tp", tag="tp")
+            turn[0] = 1 - turn[0]
+            pool, tag = ((psum_q, "q"), (psum_r, "r"))[turn[0]]
+            bank = pool.tile([P, 512], F32, name="tp", tag=tag)
             for jj in range(2):
                 for u in range(2):
                     col = (2 * jj + u) * P
@@ -86,8 +88,8 @@ def tile_sketchgcn_pa_t_kernel(tc, nf_mats, conv_mats, W1, b1, c1, out):
             else:
                 nc.scalar.copy(out=dst, in_=src)
 
-        def regroup(dst, src):
-            nc.vector.tensor_copy(
+        def regroup(copy, dst, src):
+            copy(
                 out=dst.rearrange("p (c i t) -> p c t i", i=4, t=4),
                 in_=src.rearrange("p (t c i) -> p c t i", t=4, i=4),
             )
@@ -121,20 +123,20 @@ def tile_sketchgcn_pa_t_kernel(tc, nf_mats, conv_mats, W1, b1, c1, out):
                 in_=w_grp[:, g * 2048 : (g + 1) * 2048],
             )
 
+        regroup(nc.scalar.copy, w_grp[:, 0:2048], w_raw[:, 0:2048])
+        regroup(nc.vector.tensor_copy, w_grp[:, 2048:4096], w_raw[:, 2048:4096])
+        w_quant(1)
+        w_quant(0)
         nf_half(0)
-        regroup(w_grp[:, 0:2048], w_raw[:, 0:2048])
         nf_quant(0)
         nf_half(1)
-        w_quant(0)
-        regroup(w_grp[:, 2048:4096], w_raw[:, 2048:4096])
         nf_quant(1)
-        w_quant(1)
 
-        pc = psum_z.tile([P, 512], F32, name="pc", tag="z")
+        pc = psum_h.tile([P, 512], F32, name="pc", tag="h")
         nc.tensor.matmul(out=pc[:, 0:32], lhsT=ones[:], rhs=cz[:], start=True, stop=True)
         cf = const.tile([P, 32], F32, name="cf")
         nc.scalar.activation(out=cf[:], in_=pc[:, 0:32], func=ACT.Identity)
-        pb = psum_z.tile([P, 512], F32, name="pb", tag="z")
+        pb = psum_h.tile([P, 512], F32, name="pb", tag="h")
         nc.tensor.matmul(out=pb[:], lhsT=ones[:], rhs=bz[:], start=True, stop=True)
         b1f = const.tile([P, C_H], F32, name="b1f")
         nc.scalar.copy(out=b1f[:], in_=pb[:])
@@ -152,28 +154,22 @@ def tile_sketchgcn_pa_t_kernel(tc, nf_mats, conv_mats, W1, b1, c1, out):
                 cc = codep.tile([P, 1024], U32, name="cc%d" % g, tag="cc", align_bytes=64)
                 sc = codep.tile([P, 1024], U8, name="sc%d" % g, tag="sc", align_bytes=64)
                 codes[g] = (cc, sc)
-            if b % 2 == 0:
-                grp = grpp.tile([P, 2048], BF16, name="grp", tag="grp", align_bytes=64)
-                groups[k // 2] = grp
-            grp_words = groups[k // 2][:].bitcast(F32)
+            if b == 0:
+                groups[g] = grpp.tile([P, 4096], BF16, name="grp", tag="grp", align_bytes=64)
+            grp_words = groups[g][:].bitcast(F32)
             words = conv_sb[g][:].bitcast(F32)
             j0 = 2 * b
-            lo = (b % 2) * 512
-            transpose_bank(words, [j0 * 256, (j0 + 1) * 256], grp_words[:, lo : lo + 512], "S")
-
-        def quantise_half(r):
-            g = r // 2
-            hh = r % 2
-            cc, sc = codes[g]
-            nc.vector.quantize_mx(
-                out=cc[:, hh * 512 : (hh + 1) * 512].bitcast(FP8X4),
-                scales=sc[:, hh * 512 : (hh + 1) * 512],
-                in_=groups[r][:],
+            transpose_bank(
+                words, [j0 * 256, (j0 + 1) * 256], grp_words[:, b * 512 : (b + 1) * 512], "V" if k in VCOPY else "S"
             )
 
-        prep_bank(0)
-        prep_bank(1)
-        quantise_half(0)
+        def quantise(g, first=0, last=4):
+            cc, sc = codes[g]
+            cols = slice(first * 256, last * 256)
+            nc.vector.quantize_mx(
+                out=cc[:, cols].bitcast(FP8X4), scales=sc[:, cols],
+                in_=groups[g][:, first * 1024 : last * 1024],
+            )
 
         h_grp = const.tile([P, 4 * C_H], BF16, name="h_grp", align_bytes=64)
         h_codes = const.tile([P, C_H], U32, name="h_codes", align_bytes=64)
@@ -186,8 +182,10 @@ def tile_sketchgcn_pa_t_kernel(tc, nf_mats, conv_mats, W1, b1, c1, out):
                 in_=h_grp[:, b * 512 : (b + 1) * 512],
             )
 
+        prep_bank(0)
+        prep_bank(1)
         for b in range(4):
-            acc = psum_z.tile([P, 512], F32, name="acc", tag="z")
+            acc = psum_h.tile([P, 512], F32, name="acc", tag="h")
             for j in range(4):
                 for g in range(2):
                     s = (j // 2) * 4 + g * 2 + (j % 2)
@@ -207,24 +205,26 @@ def tile_sketchgcn_pa_t_kernel(tc, nf_mats, conv_mats, W1, b1, c1, out):
                 in1=b1f[:, b * P : (b + 1) * P].unsqueeze(2).to_broadcast([P, P, 4]),
                 op=ALU.add,
             )
+            prep_bank(b + 2)
             if b >= 1:
                 h_quant(b - 1)
+            if b == 0:
+                quantise(0, 0, 2)
+            if b == 2:
+                quantise(0, 2, 4)
         h_quant(3)
-
-        for k in range(2, LEAD):
-            prep_bank(k)
-            if k % 2 == 1:
-                quantise_half(k // 2)
+        prep_bank(6)
+        prep_bank(7)
 
         halves = [slice(0, 512), slice(512, 1024)]
         state = {}
 
-        def multiply(i):
+        def multiply(i, pool, tag):
             cc, sc = codes[i // 4]
             banks = []
             for jj in range(2):
                 j = 2 * (i % 4) + jj
-                z = psum_z.tile([P, 512], F32, name="z", tag="z")
+                z = pool.tile([P, 512], F32, name="z", tag=tag)
                 nc.tensor.matmul_mx(
                     out=z[:],
                     lhsT=cc[:, j * P : (j + 1) * P].bitcast(FP8X4),
@@ -243,54 +243,67 @@ def tile_sketchgcn_pa_t_kernel(tc, nf_mats, conv_mats, W1, b1, c1, out):
                     out=tu[:, halves[jj]], in_=banks[jj][:], func=ACT.Identity, bias=c1s, scale=c2
                 )
 
-        def start_pair(i):
-            kind = KINDS[i % len(KINDS)]
-            banks = multiply(i)
+        def store(i, o):
+            b = i % 4
+            nc.sync.dma_start(out=out_v[i // 4][:, b * 1024 : (b + 1) * 1024], in_=o[:])
+
+        def store(i, o):
+            b = i % 4
+            nc.sync.dma_start(out=out_v[i // 4][:, b * 1024 : (b + 1) * 1024], in_=o[:])
+
+        def start_h(i):
+            banks = multiply(i, psum_h, "h")
             tu = work.tile([P, 1024], F32, name="tu", tag="tu")
-            if kind == "H":
-                affine(tu, banks)
-            else:
-                zs = work.tile([P, 1024], F32, name="zs", tag="zs")
-                for jj in range(2):
-                    nc.scalar.copy(out=zs[:, halves[jj]], in_=banks[jj][:])
-                if kind == "Q":
-                    affine(tu, banks)
-                else:
-                    nc.gpsimd.tensor_scalar(
-                        out=tu[:], in0=zs[:], scalar1=c2, scalar2=c1s, op0=ALU.mult, op1=ALU.add
-                    )
-                nc.gpsimd.tensor_tensor(out=tu[:], in0=tu[:], in1=zs[:], op=ALU.mult)
+            affine(tu, banks)
             state[i] = (tu, banks)
 
-        def finish_pair(i):
-            kind = KINDS[i % len(KINDS)]
+        def finish_h(i):
             tu, banks = state[i]
-            if kind != "H":
-                banks = multiply(i)
             o = outp.tile([P, 1024], F32, name="o", tag="o")
-            if kind == "H":
-                for jj in range(2):
-                    nc.vector.tensor_tensor(
-                        out=tu[:, halves[jj]], in0=tu[:, halves[jj]], in1=banks[jj][:], op=ALU.mult
-                    )
+            for jj in range(2):
+                nc.vector.tensor_tensor(
+                    out=tu[:, halves[jj]], in0=tu[:, halves[jj]], in1=banks[jj][:], op=ALU.mult
+                )
             for jj in range(2):
                 nc.vector.scalar_tensor_tensor(
                     out=o[:, halves[jj]], in0=tu[:, halves[jj]], scalar=c0, in1=banks[jj][:],
                     op0=ALU.add, op1=ALU.mult,
                 )
-            b = i % 4
-            nc.sync.dma_start(out=out_v[i // 4][:, b * 1024 : (b + 1) * 1024], in_=o[:])
+            store(i, o)
 
-        for i in range(NPAIRS + VDELAY):
-            k = LEAD + i
-            if k < NPAIRS:
-                prep_bank(k)
-            if i < NPAIRS:
-                start_pair(i)
-                if KINDS[i % len(KINDS)] == "H":
-                    finish_pair(i)
-            d = i - VDELAY
-            if d >= 0 and KINDS[d % len(KINDS)] != "H":
-                finish_pair(d)
-            if k < NPAIRS and k % 2 == 1:
-                quantise_half(k // 2)
+        def start_q(i):
+            banks = multiply(i, psum_q, "q")
+            zs = work.tile([P, 1024], F32, name="zs", tag="zs")
+            tg = work.tile([P, 1024], F32, name="tg", tag="tg")
+            for jj in range(2):
+                nc.scalar.copy(out=zs[:, halves[jj]], in_=banks[jj][:])
+                nc.scalar.activation(
+                    out=tg[:, halves[jj]], in_=banks[jj][:], func=ACT.Identity, bias=c1s, scale=c2
+                )
+            nc.gpsimd.tensor_tensor(out=tg[:], in0=tg[:], in1=zs[:], op=ALU.mult)
+            state[i] = tg
+
+        def finish_q(i):
+            tg = state[i]
+            banks = multiply(i, psum_r, "r")
+            o = outp.tile([P, 1024], F32, name="o", tag="o")
+            for jj in range(2):
+                nc.vector.scalar_tensor_tensor(
+                    out=o[:, halves[jj]], in0=tg[:, halves[jj]], scalar=c0, in1=banks[jj][:],
+                    op0=ALU.add, op1=ALU.mult,
+                )
+            store(i, o)
+
+        for k in range(8, NPAIRS):
+            prep_bank(k)
+            if k % 4 == 0:
+                quantise(k // 4 - 1)
+        start_q(0)
+        start_h(1)
+        quantise(CHUNKS - 1)
+        for i in range(0, NPAIRS, 2):
+            if i + 2 < NPAIRS:
+                start_q(i + 2)
+                start_h(i + 3)
+            finish_h(i + 1)
+            finish_q(i)

@@ -18,7 +18,18 @@ FLOPS = 2 * N * C_IN * C_H + 2 * NT * N * C_H
 CHUNKS = 8
 TILES = 8
 NPAIRS = 32
-VCOPY = (11, 19, 27)
+VCOPY = ()
+QPOS = 0
+HPOS = 1
+PATTERN = "QH"
+TAIL = 0
+QD = 1
+KD = 2
+HD = 12
+DN = 256
+WFROM = 8
+NFW = 256
+FIRST = 0
 
 
 def tile_sketchgcn_pa_t_kernel(tc, nf_mats, conv_mats, W1, b1, c1, out):
@@ -37,12 +48,14 @@ def tile_sketchgcn_pa_t_kernel(tc, nf_mats, conv_mats, W1, b1, c1, out):
 
         ident = const.tile([P, P], F32, name="ident")
         make_identity(nc, ident[:])
-        cz = const.tile([P, 32], BF16, name="cz")
-        nc.vector.memset(cz[:], 0.0)
-        bz = const.tile([P, C_H], BF16, name="bz")
-        nc.vector.memset(bz[:], 0.0)
         ones = const.tile([P, P], BF16, name="ones")
         nc.vector.memset(ones[:], 1.0)
+        cz = const.tile([P, 32], BF16, name="cz")
+        nc.vector.memset(cz[:], 0.0)
+        zeros = const.tile([P, 512], BF16, name="zeros")
+        nc.vector.memset(zeros[:], 0.0)
+        bz = const.tile([P, C_H], BF16, name="bz")
+        nc.vector.memset(bz[:], 0.0)
         nf_sb = const.tile([P, 4 * C_IN], BF16, name="nf_sb")
         nf_v = nf_mats.rearrange("(u p e) k -> p u (e k)", u=2, p=P, e=2)
         w_raw = const.tile([P, 4 * 2 * C_H], BF16, name="w_raw")
@@ -69,10 +82,21 @@ def tile_sketchgcn_pa_t_kernel(tc, nf_mats, conv_mats, W1, b1, c1, out):
 
         turn = [0]
 
-        def transpose_bank(src_words, offs, dst_words, engine):
+        def keep_warm(bank, columns):
+            nc.tensor.matmul(
+                out=bank[:, 0:columns], lhsT=ones[:], rhs=zeros[:, 0:columns], start=True, stop=True
+            )
+
+        for i in range(HD):
+            bank = psum_q.tile([P, 512], F32, name="wu", tag="q")
+            keep_warm(bank, 512)
+
+        def transpose_bank(src_words, offs, dst_words, engine, warm):
             turn[0] = 1 - turn[0]
             pool, tag = ((psum_q, "q"), (psum_r, "r"))[turn[0]]
             bank = pool.tile([P, 512], F32, name="tp", tag=tag)
+            if warm > 0:
+                keep_warm(bank, warm)
             for jj in range(2):
                 for u in range(2):
                     col = (2 * jj + u) * P
@@ -107,7 +131,7 @@ def tile_sketchgcn_pa_t_kernel(tc, nf_mats, conv_mats, W1, b1, c1, out):
             for g in range(2):
                 offs = [(2 * jp + jj) * 512 + g * 256 for jj in range(2)]
                 s0 = jp * 4 + g * 2
-                transpose_bank(nf_words, offs, nf_grp_words[:, s0 * 256 : s0 * 256 + 512], "S")
+                transpose_bank(nf_words, offs, nf_grp_words[:, s0 * 256 : s0 * 256 + 512], "S", NFW)
 
         def nf_quant(jp):
             nc.vector.quantize_mx(
@@ -160,7 +184,8 @@ def tile_sketchgcn_pa_t_kernel(tc, nf_mats, conv_mats, W1, b1, c1, out):
             words = conv_sb[g][:].bitcast(F32)
             j0 = 2 * b
             transpose_bank(
-                words, [j0 * 256, (j0 + 1) * 256], grp_words[:, b * 512 : (b + 1) * 512], "V" if k in VCOPY else "S"
+                words, [j0 * 256, (j0 + 1) * 256], grp_words[:, b * 512 : (b + 1) * 512], "V" if k in VCOPY else "S",
+                DN if k >= WFROM else 0
             )
 
         def quantise(g, first=0, last=4):
@@ -213,8 +238,6 @@ def tile_sketchgcn_pa_t_kernel(tc, nf_mats, conv_mats, W1, b1, c1, out):
             if b == 2:
                 quantise(0, 2, 4)
         h_quant(3)
-        prep_bank(6)
-        prep_bank(7)
 
         halves = [slice(0, 512), slice(512, 1024)]
         state = {}
@@ -271,19 +294,24 @@ def tile_sketchgcn_pa_t_kernel(tc, nf_mats, conv_mats, W1, b1, c1, out):
                 )
             store(i, o)
 
-        def start_q(i):
+        def start_g(i, kind):
             banks = multiply(i, psum_q, "q")
             zs = work.tile([P, 1024], F32, name="zs", tag="zs")
             tg = work.tile([P, 1024], F32, name="tg", tag="tg")
             for jj in range(2):
                 nc.scalar.copy(out=zs[:, halves[jj]], in_=banks[jj][:])
-                nc.scalar.activation(
-                    out=tg[:, halves[jj]], in_=banks[jj][:], func=ACT.Identity, bias=c1s, scale=c2
+                if kind == "Q":
+                    nc.scalar.activation(
+                        out=tg[:, halves[jj]], in_=banks[jj][:], func=ACT.Identity, bias=c1s, scale=c2
+                    )
+            if kind == "K":
+                nc.gpsimd.tensor_scalar(
+                    out=tg[:], in0=zs[:], scalar1=c2, scalar2=c1s, op0=ALU.mult, op1=ALU.add
                 )
             nc.gpsimd.tensor_tensor(out=tg[:], in0=tg[:], in1=zs[:], op=ALU.mult)
             state[i] = tg
 
-        def finish_q(i):
+        def finish_g(i):
             tg = state[i]
             banks = multiply(i, psum_r, "r")
             o = outp.tile([P, 1024], F32, name="o", tag="o")
@@ -294,16 +322,35 @@ def tile_sketchgcn_pa_t_kernel(tc, nf_mats, conv_mats, W1, b1, c1, out):
                 )
             store(i, o)
 
-        for k in range(8, NPAIRS):
-            prep_bank(k)
-            if k % 4 == 0:
-                quantise(k // 4 - 1)
-        start_q(0)
-        start_h(1)
+        start_h(0)
+        prep_bank(6)
+        prep_bank(7)
+        for g in range(1, CHUNKS):
+            for b in range(4):
+                if g > 1:
+                    prep_bank(4 * g + b)
+                if b == HPOS:
+                    start_h(g)
+                if b == QPOS and g > 1:
+                    quantise(g - 1)
+            finish_h(g - 1)
+        order = list(range(CHUNKS, NPAIRS))
+        kinds = [PATTERN[i % len(PATTERN)] for i in range(len(order) - TAIL)] + ["H"] * TAIL
+
+        def start(n):
+            if kinds[n] == "H":
+                start_h(order[n])
+            else:
+                start_g(order[n], kinds[n])
+
+        start(0)
         quantise(CHUNKS - 1)
-        for i in range(0, NPAIRS, 2):
-            if i + 2 < NPAIRS:
-                start_q(i + 2)
-                start_h(i + 3)
-            finish_h(i + 1)
-            finish_q(i)
+        finish_h(CHUNKS - 1)
+        for n in range(len(order) + 2):
+            if n + 1 < len(order):
+                start(n + 1)
+            if n < len(order) and kinds[n] == "H":
+                finish_h(order[n])
+            for kind, delay in (("Q", QD), ("K", KD)):
+                if 0 <= n - delay < len(order) and kinds[n - delay] == kind:
+                    finish_g(order[n - delay])

@@ -25,10 +25,10 @@ PATTERN = "QH"
 TAIL = 0
 QD = 1
 KD = 2
-HD = 12
-DN = 256
+HD = 0
+DN = 0
 WFROM = 8
-NFW = 256
+NFW = 0
 FIRST = 0
 
 
@@ -52,8 +52,6 @@ def tile_sketchgcn_pa_t_kernel(tc, nf_mats, conv_mats, W1, b1, c1, out):
         nc.vector.memset(ones[:], 1.0)
         cz = const.tile([P, 32], BF16, name="cz")
         nc.vector.memset(cz[:], 0.0)
-        zeros = const.tile([P, 512], BF16, name="zeros")
-        nc.vector.memset(zeros[:], 0.0)
         bz = const.tile([P, C_H], BF16, name="bz")
         nc.vector.memset(bz[:], 0.0)
         nf_sb = const.tile([P, 4 * C_IN], BF16, name="nf_sb")
@@ -82,21 +80,10 @@ def tile_sketchgcn_pa_t_kernel(tc, nf_mats, conv_mats, W1, b1, c1, out):
 
         turn = [0]
 
-        def keep_warm(bank, columns):
-            nc.tensor.matmul(
-                out=bank[:, 0:columns], lhsT=ones[:], rhs=zeros[:, 0:columns], start=True, stop=True
-            )
-
-        for i in range(HD):
-            bank = psum_q.tile([P, 512], F32, name="wu", tag="q")
-            keep_warm(bank, 512)
-
         def transpose_bank(src_words, offs, dst_words, engine, warm):
             turn[0] = 1 - turn[0]
             pool, tag = ((psum_q, "q"), (psum_r, "r"))[turn[0]]
             bank = pool.tile([P, 512], F32, name="tp", tag=tag)
-            if warm > 0:
-                keep_warm(bank, warm)
             for jj in range(2):
                 for u in range(2):
                     col = (2 * jj + u) * P

@@ -21,15 +21,17 @@ NPAIRS = 32
 VCOPY = ()
 QPOS = 0
 HPOS = 1
-PATTERN = "QH"
+EARLY = 8
+Q0A = 0
+Q0B = 9
+WEAVE = ((0, 1), (), (2, 3), (), (4, 5), (6, 7))
+SPLIT = 2
+WSPLIT = 512
+PATTERN = 3 * "FHHQHQH" + "QHQ"
 TAIL = 0
-QD = 1
+QD = 3
 KD = 2
-HD = 0
-DN = 0
-WFROM = 8
-NFW = 0
-FIRST = 0
+FD = 5
 
 
 def tile_sketchgcn_pa_t_kernel(tc, nf_mats, conv_mats, W1, b1, c1, out):
@@ -39,8 +41,8 @@ def tile_sketchgcn_pa_t_kernel(tc, nf_mats, conv_mats, W1, b1, c1, out):
         convp = ctx.enter_context(tc.tile_pool(name="convp", bufs=CHUNKS))
         grpp = ctx.enter_context(tc.tile_pool(name="grpp", bufs=2))
         codep = ctx.enter_context(tc.tile_pool(name="codep", bufs=CHUNKS))
-        work = ctx.enter_context(tc.tile_pool(name="work", bufs=3))
-        outp = ctx.enter_context(tc.tile_pool(name="outp", bufs=4))
+        work = ctx.enter_context(tc.tile_pool(name="work", bufs=4))
+        outp = ctx.enter_context(tc.tile_pool(name="outp", bufs=3))
         psum_h = ctx.enter_context(tc.psum_pool(name="psum_h", bufs=4))
         psum_q = ctx.enter_context(tc.psum_pool(name="psum_q", bufs=2))
         psum_r = ctx.enter_context(tc.psum_pool(name="psum_r", bufs=2))
@@ -63,7 +65,6 @@ def tile_sketchgcn_pa_t_kernel(tc, nf_mats, conv_mats, W1, b1, c1, out):
                 out=w_raw[:, u * 2048 : (u + 1) * 2048].rearrange("q (a x) -> q a x", a=2),
                 in_=w_v[:, 2 * u : 2 * u + 2, :],
             )
-        for u in range(2):
             nc.sync.dma_start(out=nf_sb[:, u * 2048 : (u + 1) * 2048], in_=nf_v[:, u, :])
         nc.sync.dma_start(out=cz[0:1, 0:3], in_=c1.rearrange("(o c) -> o c", o=1))
         nc.sync.dma_start(out=bz[0:1, :], in_=b1.rearrange("(o c) -> o c", o=1))
@@ -80,7 +81,7 @@ def tile_sketchgcn_pa_t_kernel(tc, nf_mats, conv_mats, W1, b1, c1, out):
 
         turn = [0]
 
-        def transpose_bank(src_words, offs, dst_words, engine, warm):
+        def transpose_bank(src_words, offs, dst_words, engine):
             turn[0] = 1 - turn[0]
             pool, tag = ((psum_q, "q"), (psum_r, "r"))[turn[0]]
             bank = pool.tile([P, 512], F32, name="tp", tag=tag)
@@ -99,10 +100,14 @@ def tile_sketchgcn_pa_t_kernel(tc, nf_mats, conv_mats, W1, b1, c1, out):
             else:
                 nc.scalar.copy(out=dst, in_=src)
 
-        def regroup(copy, dst, src):
+        def regroup(copy, g, lo, hi):
+            half = slice(g * 2048, (g + 1) * 2048)
+            src = w_raw[:, half].rearrange("p (t c) -> p t c", t=4)[:, :, lo:hi]
             copy(
-                out=dst.rearrange("p (c i t) -> p c t i", i=4, t=4),
-                in_=src.rearrange("p (t c i) -> p c t i", t=4, i=4),
+                out=w_grp[:, g * 2048 + 4 * lo : g * 2048 + 4 * hi].rearrange(
+                    "p (c i t) -> p c t i", i=4, t=4
+                ),
+                in_=src.rearrange("p t (c i) -> p c t i", i=4),
             )
 
         nf_words = nf_sb[:].bitcast(F32)
@@ -118,7 +123,7 @@ def tile_sketchgcn_pa_t_kernel(tc, nf_mats, conv_mats, W1, b1, c1, out):
             for g in range(2):
                 offs = [(2 * jp + jj) * 512 + g * 256 for jj in range(2)]
                 s0 = jp * 4 + g * 2
-                transpose_bank(nf_words, offs, nf_grp_words[:, s0 * 256 : s0 * 256 + 512], "S", NFW)
+                transpose_bank(nf_words, offs, nf_grp_words[:, s0 * 256 : s0 * 256 + 512], "S")
 
         def nf_quant(jp):
             nc.vector.quantize_mx(
@@ -134,12 +139,14 @@ def tile_sketchgcn_pa_t_kernel(tc, nf_mats, conv_mats, W1, b1, c1, out):
                 in_=w_grp[:, g * 2048 : (g + 1) * 2048],
             )
 
-        regroup(nc.scalar.copy, w_grp[:, 0:2048], w_raw[:, 0:2048])
-        regroup(nc.vector.tensor_copy, w_grp[:, 2048:4096], w_raw[:, 2048:4096])
-        w_quant(1)
+        regroup(nc.vector.tensor_copy, 0, 0, 512)
         w_quant(0)
         nf_half(0)
+        regroup(nc.vector.tensor_copy, 1, 0, WSPLIT)
+        if WSPLIT < 512:
+            regroup(nc.scalar.copy, 1, WSPLIT, 512)
         nf_quant(0)
+        w_quant(1)
         nf_half(1)
         nf_quant(1)
 
@@ -171,8 +178,7 @@ def tile_sketchgcn_pa_t_kernel(tc, nf_mats, conv_mats, W1, b1, c1, out):
             words = conv_sb[g][:].bitcast(F32)
             j0 = 2 * b
             transpose_bank(
-                words, [j0 * 256, (j0 + 1) * 256], grp_words[:, b * 512 : (b + 1) * 512], "V" if k in VCOPY else "S",
-                DN if k >= WFROM else 0
+                words, [j0 * 256, (j0 + 1) * 256], grp_words[:, b * 512 : (b + 1) * 512], "V" if k in VCOPY else "S"
             )
 
         def quantise(g, first=0, last=4):
@@ -194,8 +200,8 @@ def tile_sketchgcn_pa_t_kernel(tc, nf_mats, conv_mats, W1, b1, c1, out):
                 in_=h_grp[:, b * 512 : (b + 1) * 512],
             )
 
-        prep_bank(0)
-        prep_bank(1)
+        for k in WEAVE[0]:
+            prep_bank(k)
         for b in range(4):
             acc = psum_h.tile([P, 512], F32, name="acc", tag="h")
             for j in range(4):
@@ -217,12 +223,13 @@ def tile_sketchgcn_pa_t_kernel(tc, nf_mats, conv_mats, W1, b1, c1, out):
                 in1=b1f[:, b * P : (b + 1) * P].unsqueeze(2).to_broadcast([P, P, 4]),
                 op=ALU.add,
             )
-            prep_bank(b + 2)
+            for k in WEAVE[b + 1]:
+                prep_bank(k)
             if b >= 1:
                 h_quant(b - 1)
-            if b == 0:
+            if b == Q0A:
                 quantise(0, 0, 2)
-            if b == 2:
+            if b == Q0B:
                 quantise(0, 2, 4)
         h_quant(3)
 
@@ -255,11 +262,10 @@ def tile_sketchgcn_pa_t_kernel(tc, nf_mats, conv_mats, W1, b1, c1, out):
 
         def store(i, o):
             b = i % 4
-            nc.sync.dma_start(out=out_v[i // 4][:, b * 1024 : (b + 1) * 1024], in_=o[:])
-
-        def store(i, o):
-            b = i % 4
-            nc.sync.dma_start(out=out_v[i // 4][:, b * 1024 : (b + 1) * 1024], in_=o[:])
+            for half in halves if i >= NPAIRS - SPLIT else (slice(0, 1024),):
+                nc.sync.dma_start(
+                    out=out_v[i // 4][:, b * 1024 + half.start : b * 1024 + half.stop], in_=o[:, half]
+                )
 
         def start_h(i):
             banks = multiply(i, psum_h, "h")
@@ -287,7 +293,7 @@ def tile_sketchgcn_pa_t_kernel(tc, nf_mats, conv_mats, W1, b1, c1, out):
             tg = work.tile([P, 1024], F32, name="tg", tag="tg")
             for jj in range(2):
                 nc.scalar.copy(out=zs[:, halves[jj]], in_=banks[jj][:])
-                if kind == "Q":
+                if kind != "K":
                     nc.scalar.activation(
                         out=tg[:, halves[jj]], in_=banks[jj][:], func=ACT.Identity, bias=c1s, scale=c2
                     )
@@ -296,6 +302,11 @@ def tile_sketchgcn_pa_t_kernel(tc, nf_mats, conv_mats, W1, b1, c1, out):
                     out=tg[:], in0=zs[:], scalar1=c2, scalar2=c1s, op0=ALU.mult, op1=ALU.add
                 )
             nc.gpsimd.tensor_tensor(out=tg[:], in0=tg[:], in1=zs[:], op=ALU.mult)
+            if kind == "F":
+                nc.gpsimd.tensor_scalar(
+                    out=tg[:], in0=tg[:], scalar1=1.0, scalar2=c0, op0=ALU.mult, op1=ALU.add
+                )
+                nc.gpsimd.tensor_tensor(out=tg[:], in0=tg[:], in1=zs[:], op=ALU.mult)
             state[i] = tg
 
         def finish_g(i):
@@ -310,18 +321,21 @@ def tile_sketchgcn_pa_t_kernel(tc, nf_mats, conv_mats, W1, b1, c1, out):
             store(i, o)
 
         start_h(0)
-        prep_bank(6)
-        prep_bank(7)
+        if Q0B == 9:
+            quantise(0, 2, 4)
+        for k in WEAVE[5]:
+            prep_bank(k)
         for g in range(1, CHUNKS):
             for b in range(4):
                 if g > 1:
                     prep_bank(4 * g + b)
-                if b == HPOS:
+                if b == HPOS and g < EARLY:
                     start_h(g)
                 if b == QPOS and g > 1:
                     quantise(g - 1)
-            finish_h(g - 1)
-        order = list(range(CHUNKS, NPAIRS))
+            if g - 1 < EARLY:
+                finish_h(g - 1)
+        order = list(range(EARLY, NPAIRS))
         kinds = [PATTERN[i % len(PATTERN)] for i in range(len(order) - TAIL)] + ["H"] * TAIL
 
         def start(n):
@@ -332,8 +346,9 @@ def tile_sketchgcn_pa_t_kernel(tc, nf_mats, conv_mats, W1, b1, c1, out):
 
         start(0)
         quantise(CHUNKS - 1)
-        finish_h(CHUNKS - 1)
-        for n in range(len(order) + 2):
+        if EARLY == CHUNKS:
+            finish_h(CHUNKS - 1)
+        for n in range(len(order) + max(QD, KD, FD)):
             if n + 1 < len(order):
                 start(n + 1)
             if n < len(order) and kinds[n] == "H":
@@ -341,3 +356,5 @@ def tile_sketchgcn_pa_t_kernel(tc, nf_mats, conv_mats, W1, b1, c1, out):
             for kind, delay in (("Q", QD), ("K", KD)):
                 if 0 <= n - delay < len(order) and kinds[n - delay] == kind:
                     finish_g(order[n - delay])
+            if 0 <= n - FD < len(order) and kinds[n - FD] == "F":
+                store(order[n - FD], state[order[n - FD]])

from contextlib import ExitStack

import concourse.mybir as mybir
from concourse.masks import make_identity

F32 = mybir.dt.float32
BF16 = mybir.dt.bfloat16
U32 = mybir.dt.uint32
U8 = mybir.dt.uint8
FP8X4 = mybir.dt.float8_e4m3fn_x4
ALU = mybir.AluOpType
ACT = mybir.ActivationFunctionType

P = 128
NT, N, C_IN, C_H = 8192, 512, 1024, 512
FLOPS = 2 * N * C_IN * C_H + 2 * NT * N * C_H

CHUNKS = 8
TILES = 8
NPAIRS = 32
VCOPY = ()
QPOS = 0
HPOS = 1
EARLY = 8
Q0A = 0
Q0B = 9
WEAVE = ((0, 1), (), (2, 3), (), (4, 5), (6, 7))
SPLIT = 2
WSPLIT = 512
PATTERN = 3 * "FHHQHQH" + "QHQ"
TAIL = 0
QD = 3
KD = 2
FD = 5


def tile_sketchgcn_pa_t_kernel(tc, nf_mats, conv_mats, W1, b1, c1, out):
    nc = tc.nc
    with ExitStack() as ctx:
        const = ctx.enter_context(tc.tile_pool(name="const", bufs=1))
        convp = ctx.enter_context(tc.tile_pool(name="convp", bufs=CHUNKS))
        grpp = ctx.enter_context(tc.tile_pool(name="grpp", bufs=2))
        codep = ctx.enter_context(tc.tile_pool(name="codep", bufs=CHUNKS))
        work = ctx.enter_context(tc.tile_pool(name="work", bufs=4))
        outp = ctx.enter_context(tc.tile_pool(name="outp", bufs=3))
        psum_h = ctx.enter_context(tc.psum_pool(name="psum_h", bufs=4))
        psum_q = ctx.enter_context(tc.psum_pool(name="psum_q", bufs=2))
        psum_r = ctx.enter_context(tc.psum_pool(name="psum_r", bufs=2))
        ctx.enter_context(tc.manual_schedule())

        ident = const.tile([P, P], F32, name="ident")
        make_identity(nc, ident[:])
        ones = const.tile([P, P], BF16, name="ones")
        nc.vector.memset(ones[:], 1.0)
        cz = const.tile([P, 32], BF16, name="cz")
        nc.vector.memset(cz[:], 0.0)
        bz = const.tile([P, C_H], BF16, name="bz")
        nc.vector.memset(bz[:], 0.0)
        nf_sb = const.tile([P, 4 * C_IN], BF16, name="nf_sb")
        nf_v = nf_mats.rearrange("(u p e) k -> p u (e k)", u=2, p=P, e=2)
        w_raw = const.tile([P, 4 * 2 * C_H], BF16, name="w_raw")
        w_v = W1.rearrange("(a q e) c -> q a (e c)", a=4, q=P, e=2)
        for u in range(2):
            nc.sync.dma_start(
                out=w_raw[:, u * 2048 : (u + 1) * 2048].rearrange("q (a x) -> q a x", a=2),
                in_=w_v[:, 2 * u : 2 * u + 2, :],
            )
            nc.sync.dma_start(out=nf_sb[:, u * 2048 : (u + 1) * 2048], in_=nf_v[:, u, :])
        nc.sync.dma_start(out=cz[0:1, 0:3], in_=c1.rearrange("(o c) -> o c", o=1))
        nc.sync.dma_start(out=bz[0:1, :], in_=b1.rearrange("(o c) -> o c", o=1))
        conv_v = conv_mats.rearrange("(g p j) n -> g p (j n)", g=CHUNKS, p=P, j=TILES)
        out_v = out.rearrange("(g p j) c -> g p (j c)", g=CHUNKS, p=P, j=TILES)
        conv_sb = []
        for g in range(CHUNKS):
            cs = convp.tile([P, TILES * N], BF16, name="conv%d" % g, tag="conv")
            parts = 2 if g == 0 else 1
            w = TILES * N // parts
            for u in range(parts):
                nc.sync.dma_start(out=cs[:, u * w : (u + 1) * w], in_=conv_v[g][:, u * w : (u + 1) * w])
            conv_sb.append(cs)

        turn = [0]

        def transpose_bank(src_words, offs, dst_words, engine):
            turn[0] = 1 - turn[0]
            pool, tag = ((psum_q, "q"), (psum_r, "r"))[turn[0]]
            bank = pool.tile([P, 512], F32, name="tp", tag=tag)
            for jj in range(2):
                for u in range(2):
                    col = (2 * jj + u) * P
                    nc.tensor.transpose(
                        bank[:, col : col + P],
                        src_words[:, offs[jj] + P * u : offs[jj] + P * (u + 1)],
                        ident[:],
                    )
            dst = dst_words.rearrange("p (jj m u) -> p jj m u", jj=2, u=2)
            src = bank[:].rearrange("p (jj u m) -> p jj m u", jj=2, u=2)
            if engine == "V":
                nc.vector.tensor_copy(out=dst, in_=src)
            else:
                nc.scalar.copy(out=dst, in_=src)

        def regroup(copy, g, lo, hi):
            half = slice(g * 2048, (g + 1) * 2048)
            src = w_raw[:, half].rearrange("p (t c) -> p t c", t=4)[:, :, lo:hi]
            copy(
                out=w_grp[:, g * 2048 + 4 * lo : g * 2048 + 4 * hi].rearrange(
                    "p (c i t) -> p c t i", i=4, t=4
                ),
                in_=src.rearrange("p t (c i) -> p c t i", i=4),
            )

        nf_words = nf_sb[:].bitcast(F32)
        nf_grp = const.tile([P, 4096], BF16, name="nf_grp", align_bytes=64)
        nf_grp_words = nf_grp[:].bitcast(F32)
        nf_codes = const.tile([P, 1024], U32, name="nf_codes", align_bytes=64)
        nf_scales = const.tile([P, 1024], U8, name="nf_scales", align_bytes=64)
        w_grp = const.tile([P, 4096], BF16, name="w_grp", align_bytes=64)
        w_codes = const.tile([P, 1024], U32, name="w_codes", align_bytes=64)
        w_scales = const.tile([P, 1024], U8, name="w_scales", align_bytes=64)

        def nf_half(jp):
            for g in range(2):
                offs = [(2 * jp + jj) * 512 + g * 256 for jj in range(2)]
                s0 = jp * 4 + g * 2
                transpose_bank(nf_words, offs, nf_grp_words[:, s0 * 256 : s0 * 256 + 512], "S")

        def nf_quant(jp):
            nc.vector.quantize_mx(
                out=nf_codes[:, jp * 512 : (jp + 1) * 512].bitcast(FP8X4),
                scales=nf_scales[:, jp * 512 : (jp + 1) * 512],
                in_=nf_grp[:, jp * 2048 : (jp + 1) * 2048],
            )

        def w_quant(g):
            nc.vector.quantize_mx(
                out=w_codes[:, g * 512 : (g + 1) * 512].bitcast(FP8X4),
                scales=w_scales[:, g * 512 : (g + 1) * 512],
                in_=w_grp[:, g * 2048 : (g + 1) * 2048],
            )

        regroup(nc.vector.tensor_copy, 0, 0, 512)
        w_quant(0)
        nf_half(0)
        regroup(nc.vector.tensor_copy, 1, 0, WSPLIT)
        if WSPLIT < 512:
            regroup(nc.scalar.copy, 1, WSPLIT, 512)
        nf_quant(0)
        w_quant(1)
        nf_half(1)
        nf_quant(1)

        pc = psum_h.tile([P, 512], F32, name="pc", tag="h")
        nc.tensor.matmul(out=pc[:, 0:32], lhsT=ones[:], rhs=cz[:], start=True, stop=True)
        cf = const.tile([P, 32], F32, name="cf")
        nc.scalar.activation(out=cf[:], in_=pc[:, 0:32], func=ACT.Identity)
        pb = psum_h.tile([P, 512], F32, name="pb", tag="h")
        nc.tensor.matmul(out=pb[:], lhsT=ones[:], rhs=bz[:], start=True, stop=True)
        b1f = const.tile([P, C_H], F32, name="b1f")
        nc.scalar.copy(out=b1f[:], in_=pb[:])
        c0 = cf[:, 0:1]
        c1s = cf[:, 1:2]
        c2 = cf[:, 2:3]

        codes = {}
        groups = {}

        def prep_bank(k):
            g = k // 4
            b = k % 4
            if b == 0:
                cc = codep.tile([P, 1024], U32, name="cc%d" % g, tag="cc", align_bytes=64)
                sc = codep.tile([P, 1024], U8, name="sc%d" % g, tag="sc", align_bytes=64)
                codes[g] = (cc, sc)
            if b == 0:
                groups[g] = grpp.tile([P, 4096], BF16, name="grp", tag="grp", align_bytes=64)
            grp_words = groups[g][:].bitcast(F32)
            words = conv_sb[g][:].bitcast(F32)
            j0 = 2 * b
            transpose_bank(
                words, [j0 * 256, (j0 + 1) * 256], grp_words[:, b * 512 : (b + 1) * 512], "V" if k in VCOPY else "S"
            )

        def quantise(g, first=0, last=4):
            cc, sc = codes[g]
            cols = slice(first * 256, last * 256)
            nc.vector.quantize_mx(
                out=cc[:, cols].bitcast(FP8X4), scales=sc[:, cols],
                in_=groups[g][:, first * 1024 : last * 1024],
            )

        h_grp = const.tile([P, 4 * C_H], BF16, name="h_grp", align_bytes=64)
        h_codes = const.tile([P, C_H], U32, name="h_codes", align_bytes=64)
        h_scales = const.tile([P, C_H], U8, name="h_scales", align_bytes=64)

        def h_quant(b):
            nc.vector.quantize_mx(
                out=h_codes[:, b * P : (b + 1) * P].bitcast(FP8X4),
                scales=h_scales[:, b * P : (b + 1) * P],
                in_=h_grp[:, b * 512 : (b + 1) * 512],
            )

        for k in WEAVE[0]:
            prep_bank(k)
        for b in range(4):
            acc = psum_h.tile([P, 512], F32, name="acc", tag="h")
            for j in range(4):
                for g in range(2):
                    s = (j // 2) * 4 + g * 2 + (j % 2)
                    cols = slice(g * 512 + b * P, g * 512 + (b + 1) * P)
                    nc.tensor.matmul_mx(
                        out=acc[:, j * P : (j + 1) * P],
                        lhsT=nf_codes[:, s * P : (s + 1) * P].bitcast(FP8X4),
                        lhsT_scale=nf_scales[:, s * P : (s + 1) * P],
                        rhs=w_codes[:, cols].bitcast(FP8X4),
                        rhs_scale=w_scales[:, cols],
                        start=(g == 0),
                        stop=(g == 1),
                    )
            nc.vector.tensor_tensor(
                out=h_grp[:, b * 512 : (b + 1) * 512].rearrange("p (c j) -> p c j", j=4),
                in0=acc[:].rearrange("p (j c) -> p c j", j=4),
                in1=b1f[:, b * P : (b + 1) * P].unsqueeze(2).to_broadcast([P, P, 4]),
                op=ALU.add,
            )
            for k in WEAVE[b + 1]:
                prep_bank(k)
            if b >= 1:
                h_quant(b - 1)
            if b == Q0A:
                quantise(0, 0, 2)
            if b == Q0B:
                quantise(0, 2, 4)
        h_quant(3)

        halves = [slice(0, 512), slice(512, 1024)]
        state = {}

        def multiply(i, pool, tag):
            cc, sc = codes[i // 4]
            banks = []
            for jj in range(2):
                j = 2 * (i % 4) + jj
                z = pool.tile([P, 512], F32, name="z", tag=tag)
                nc.tensor.matmul_mx(
                    out=z[:],
                    lhsT=cc[:, j * P : (j + 1) * P].bitcast(FP8X4),
                    lhsT_scale=sc[:, j * P : (j + 1) * P],
                    rhs=h_codes[:].bitcast(FP8X4),
                    rhs_scale=h_scales[:],
                    start=True,
                    stop=True,
                )
                banks.append(z)
            return banks

        def affine(tu, banks):
            for jj in range(2):
                nc.scalar.activation(
                    out=tu[:, halves[jj]], in_=banks[jj][:], func=ACT.Identity, bias=c1s, scale=c2
                )

        def store(i, o):
            b = i % 4
            for half in halves if i >= NPAIRS - SPLIT else (slice(0, 1024),):
                nc.sync.dma_start(
                    out=out_v[i // 4][:, b * 1024 + half.start : b * 1024 + half.stop], in_=o[:, half]
                )

        def start_h(i):
            banks = multiply(i, psum_h, "h")
            tu = work.tile([P, 1024], F32, name="tu", tag="tu")
            affine(tu, banks)
            state[i] = (tu, banks)

        def finish_h(i):
            tu, banks = state[i]
            o = outp.tile([P, 1024], F32, name="o", tag="o")
            for jj in range(2):
                nc.vector.tensor_tensor(
                    out=tu[:, halves[jj]], in0=tu[:, halves[jj]], in1=banks[jj][:], op=ALU.mult
                )
            for jj in range(2):
                nc.vector.scalar_tensor_tensor(
                    out=o[:, halves[jj]], in0=tu[:, halves[jj]], scalar=c0, in1=banks[jj][:],
                    op0=ALU.add, op1=ALU.mult,
                )
            store(i, o)

        def start_g(i, kind):
            banks = multiply(i, psum_q, "q")
            zs = work.tile([P, 1024], F32, name="zs", tag="zs")
            tg = work.tile([P, 1024], F32, name="tg", tag="tg")
            for jj in range(2):
                nc.scalar.copy(out=zs[:, halves[jj]], in_=banks[jj][:])
                if kind != "K":
                    nc.scalar.activation(
                        out=tg[:, halves[jj]], in_=banks[jj][:], func=ACT.Identity, bias=c1s, scale=c2
                    )
            if kind == "K":
                nc.gpsimd.tensor_scalar(
                    out=tg[:], in0=zs[:], scalar1=c2, scalar2=c1s, op0=ALU.mult, op1=ALU.add
                )
            nc.gpsimd.tensor_tensor(out=tg[:], in0=tg[:], in1=zs[:], op=ALU.mult)
            if kind == "F":
                nc.gpsimd.tensor_scalar(
                    out=tg[:], in0=tg[:], scalar1=1.0, scalar2=c0, op0=ALU.mult, op1=ALU.add
                )
                nc.gpsimd.tensor_tensor(out=tg[:], in0=tg[:], in1=zs[:], op=ALU.mult)
            state[i] = tg

        def finish_g(i):
            tg = state[i]
            banks = multiply(i, psum_r, "r")
            o = outp.tile([P, 1024], F32, name="o", tag="o")
            for jj in range(2):
                nc.vector.scalar_tensor_tensor(
                    out=o[:, halves[jj]], in0=tg[:, halves[jj]], scalar=c0, in1=banks[jj][:],
                    op0=ALU.add, op1=ALU.mult,
                )
            store(i, o)

        start_h(0)
        if Q0B == 9:
            quantise(0, 2, 4)
        for k in WEAVE[5]:
            prep_bank(k)
        for g in range(1, CHUNKS):
            for b in range(4):
                if g > 1:
                    prep_bank(4 * g + b)
                if b == HPOS and g < EARLY:
                    start_h(g)
                if b == QPOS and g > 1:
                    quantise(g - 1)
            if g - 1 < EARLY:
                finish_h(g - 1)
        order = list(range(EARLY, NPAIRS))
        kinds = [PATTERN[i % len(PATTERN)] for i in range(len(order) - TAIL)] + ["H"] * TAIL

        def start(n):
            if kinds[n] == "H":
                start_h(order[n])
            else:
                start_g(order[n], kinds[n])

        start(0)
        quantise(CHUNKS - 1)
        if EARLY == CHUNKS:
            finish_h(CHUNKS - 1)
        for n in range(len(order) + max(QD, KD, FD)):
            if n + 1 < len(order):
                start(n + 1)
            if n < len(order) and kinds[n] == "H":
                finish_h(order[n])
            for kind, delay in (("Q", QD), ("K", KD)):
                if 0 <= n - delay < len(order) and kinds[n - delay] == kind:
                    finish_g(order[n - delay])
            if 0 <= n - FD < len(order) and kinds[n - FD] == "F":
                store(order[n - FD], state[order[n - FD]])
